import numpy as np
import ml_dtypes


def mxq(x, axis, fmt="e4m3"):
    dtype, down = {"e4m3": (ml_dtypes.float8_e4m3fn, 7), "e5m2": (ml_dtypes.float8_e5m2, 14)}[fmt]
    v = np.moveaxis(np.asarray(x, np.float32).astype(ml_dtypes.bfloat16).astype(np.float64), axis, -1)
    blocks = v.reshape(v.shape[:-1] + (-1, 32))
    amax = np.abs(blocks).max(-1, keepdims=True)
    byte = np.maximum(np.where(amax > 0, np.frexp(amax)[1] - 1 + 127, 0) - down, 1)
    scale = np.exp2(byte - 127.0)
    codes = (blocks / scale).astype(np.float32).astype(dtype).astype(np.float64)
    return np.moveaxis((codes * scale).reshape(v.shape), -1, axis)


WIDE = False


def mx_kscale(k):
    if not WIDE:
        return np.ones(k)
    levels = np.array([10, -10, 5, -5, 0])
    a = np.random.permutation(np.resize(levels, k // 512 * 4)).reshape(k // 512, 4)
    idx = np.arange(k)
    return np.exp2(a[idx // 512, idx % 128 // 32])


BF16 = ml_dtypes.bfloat16


def bf(x):
    return np.asarray(x, np.float32).astype(BF16)


def f64(x):
    return np.asarray(x).astype(np.float64)


B, N, IN_DIM, UNITS, K = 2, 1024, 128, 128, 3
F = IN_DIM + UNITS


def setup_inputs():
    s = mx_kscale(N)
    adj = np.random.standard_normal((N, N)) * 0.5 / np.sqrt(N) * s[None, :] / s[:, None]
    x0 = np.random.standard_normal((B, N, F)) / s[None, :, None]
    return {"adj": bf(adj), "x0": bf(x0)}


def reference(adj, x0):
    aq = mxq(f64(adj), 1, "e4m3")
    x0 = f64(x0)
    x1 = aq @ mxq(x0, 1, "e4m3")
    x2 = 2.0 * (aq @ mxq(x1, 1, "e4m3")) - x0
    return x1, x2

@@ -1,0 +1,164 @@
+import concourse.mybir as mybir
+from concourse.masks import make_identity
+
+BF16 = mybir.dt.bfloat16
+F32 = mybir.dt.float32
+U32 = mybir.dt.uint32
+U8 = mybir.dt.uint8
+FP8X4 = mybir.dt.float8_e4m3fn_x4
+
+P = 128
+PACK = 4
+PAIR = 2
+NODES = 1024
+BATCH = 2
+FEATURES = 256
+PASSES = NODES // (P * PACK)
+CHUNKS = NODES // (P * PAIR)
+CHUNKS_PER_PASS = CHUNKS // PASSES
+WORDS = NODES // PAIR
+
+FLOPS = 2 * 2 * NODES * NODES * BATCH * FEATURES
+
+
+def tile_gts_gcgrucell_pa_kernel(tc, adj, x0, out_0, out_1):
+    nc = tc.nc
+    with tc.tile_pool(name="keep", bufs=1) as keep, tc.psum_pool(name="psum", bufs=8) as psum:
+        identity = keep.tile([P, P], F32)
+        x0_rows, x1_rows, x2_rows = [], [], []
+        x0_grouped, x0_codes, x0_scales = [], [], []
+        x1_grouped, x1_codes, x1_scales = [], [], []
+        for b in range(BATCH):
+            x0_rows.append(keep.tile([P, CHUNKS, PAIR, FEATURES], BF16, name="x0_rows%d" % b))
+            x1_rows.append(keep.tile([P, CHUNKS, PAIR, FEATURES], F32, name="x1_rows%d" % b))
+            x2_rows.append(keep.tile([P, CHUNKS, PAIR, FEATURES], F32, name="x2_rows%d" % b))
+            grouped_shape = [P, PASSES, FEATURES, PACK]
+            x0_grouped.append(keep.tile(grouped_shape, BF16, name="x0_grouped%d" % b, align_bytes=64))
+            x1_grouped.append(keep.tile(grouped_shape, BF16, name="x1_grouped%d" % b, align_bytes=64))
+            x0_codes.append(keep.tile([P, PASSES, FEATURES], U32, name="x0_codes%d" % b, align_bytes=64))
+            x0_scales.append(keep.tile([P, PASSES, FEATURES], U8, name="x0_scales%d" % b, align_bytes=64))
+            x1_codes.append(keep.tile([P, PASSES, FEATURES], U32, name="x1_codes%d" % b, align_bytes=64))
+            x1_scales.append(keep.tile([P, PASSES, FEATURES], U8, name="x1_scales%d" % b, align_bytes=64))
+        adj_rows, adj_grouped, adj_codes, adj_scales = [], [], [], []
+        for c in range(CHUNKS):
+            adj_rows.append(keep.tile([P, PAIR * NODES], BF16, name="adj_rows%d" % c))
+            adj_grouped.append(
+                keep.tile([P, PAIR, PASSES * P * PACK], BF16, name="adj_grouped%d" % c, align_bytes=64)
+            )
+            adj_codes.append(keep.tile([P, PAIR, PASSES, P], U32, name="adj_codes%d" % c, align_bytes=64))
+            adj_scales.append(keep.tile([P, PAIR, PASSES, P], U8, name="adj_scales%d" % c, align_bytes=64))
+
+        def load_x0(b):
+            nc.sync.dma_start(
+                out=x0_rows[b][:].rearrange("p c e f -> p c (e f)"),
+                in_=x0[b].rearrange("(c p e) f -> p c (e f)", p=P, e=PAIR),
+            )
+
+        def load_adj(c):
+            nc.sync.dma_start(
+                out=adj_rows[c][:],
+                in_=adj[c * P * PAIR : (c + 1) * P * PAIR, :].rearrange("(p e) k -> p (e k)", e=PAIR),
+            )
+
+        def store(out, rows, b, c):
+            nc.sync.dma_start(
+                out=out[b, c * P * PAIR : (c + 1) * P * PAIR, :].rearrange("(p e) f -> p (e f)", e=PAIR),
+                in_=rows[b][:, c].rearrange("p e f -> p (e f)"),
+            )
+
+        def regroup(grouped, rows, b, g):
+            chunks = slice(g * CHUNKS_PER_PASS, (g + 1) * CHUNKS_PER_PASS)
+            nc.vector.tensor_copy(
+                out=grouped[b][:, g], in_=rows[b][:, chunks].rearrange("p u e f -> p f (u e)")
+            )
+
+        def quantise(grouped, codes, scales):
+            nc.vector.quantize_mx(out=codes.bitcast(FP8X4), scales=scales, in_=grouped)
+
+        def prepare_x0(b):
+            for g in range(PASSES):
+                regroup(x0_grouped, x0_rows, b, g)
+            quantise(
+                x0_grouped[b][:].rearrange("p g f t -> p (g f t)"),
+                x0_codes[b][:].rearrange("p g f -> p (g f)"),
+                x0_scales[b][:].rearrange("p g f -> p (g f)"),
+            )
+
+        def transpose_adj(c):
+            words = adj_rows[c][:].bitcast(F32)
+            for e in range(PAIR):
+                flipped = psum.tile([P, CHUNKS, P], F32, tag="bank")
+                for j in range(CHUNKS):
+                    first = e * WORDS + j * P
+                    nc.tensor.transpose(flipped[:, j, :], words[:, first : first + P], identity[:])
+                nc.scalar.copy(
+                    out=adj_grouped[c][:, e].bitcast(F32).rearrange(
+                        "p (g r u) -> p g r u", g=PASSES, u=CHUNKS_PER_PASS
+                    ),
+                    in_=flipped[:].rearrange("p (g u) r -> p g r u", u=CHUNKS_PER_PASS),
+                )
+                quantise(
+                    adj_grouped[c][:, e],
+                    adj_codes[c][:, e].rearrange("p g r -> p (g r)"),
+                    adj_scales[c][:, e].rearrange("p g r -> p (g r)"),
+                )
+
+        def multiply(c, codes, scales):
+            product = psum.tile([P, PAIR, FEATURES], F32, tag="bank")
+            for e in range(PAIR):
+                for g in range(PASSES):
+                    nc.tensor.matmul_mx(
+                        out=product[:, e, :],
+                        lhsT=adj_codes[c][:, e, g, :].bitcast(FP8X4),
+                        lhsT_scale=adj_scales[c][:, e, g, :],
+                        rhs=codes[:, g, :].bitcast(FP8X4),
+                        rhs_scale=scales[:, g, :],
+                        start=(g == 0),
+                        stop=(g == PASSES - 1),
+                    )
+            return product
+
+        def first_product(b, c):
+            product = multiply(c, x0_codes[b], x0_scales[b])
+            nc.scalar.copy(out=x1_rows[b][:, c], in_=product[:])
+            store(out_0, x1_rows, b, c)
+            if c % CHUNKS_PER_PASS == CHUNKS_PER_PASS - 1:
+                g = c // CHUNKS_PER_PASS
+                regroup(x1_grouped, x1_rows, b, g)
+                quantise(
+                    x1_grouped[b][:, g].rearrange("p f t -> p (f t)"), x1_codes[b][:, g], x1_scales[b][:, g]
+                )
+
+        def second_product(b, c):
+            product = multiply(c, x1_codes[b], x1_scales[b])
+            nc.vector.scalar_tensor_tensor(
+                out=x2_rows[b][:, c],
+                in0=product[:],
+                scalar=2.0,
+                in1=x0_rows[b][:, c],
+                op0=mybir.AluOpType.mult,
+                op1=mybir.AluOpType.subtract,
+            )
+            store(out_1, x2_rows, b, c)
+
+        load_x0(0)
+        load_adj(0)
+        load_adj(1)
+        load_x0(1)
+        load_adj(2)
+        load_adj(3)
+        make_identity(nc, identity[:])
+
+        prepare_x0(0)
+        transpose_adj(0)
+        transpose_adj(1)
+        prepare_x0(1)
+        for c in range(CHUNKS):
+            first_product(0, c)
+            if c + 2 < CHUNKS:
+                transpose_adj(c + 2)
+        for c in range(CHUNKS):
+            first_product(1, c)
+        for b in range(BATCH):
+            for c in range(CHUNKS):
+                second_product(b, c)

@@ -141,24 +141,25 @@ def tile_gts_gcgrucell_pa_kernel(tc, adj, x0, out_0, out_1):
             )
             store(out_1, x2_rows, b, c)
 
-        load_x0(0)
-        load_adj(0)
-        load_adj(1)
-        load_x0(1)
-        load_adj(2)
-        load_adj(3)
-        make_identity(nc, identity[:])
+        with tc.manual_schedule():
+            load_x0(0)
+            load_adj(0)
+            load_adj(1)
+            load_x0(1)
+            load_adj(2)
+            load_adj(3)
+            make_identity(nc, identity[:])
 
-        prepare_x0(0)
-        transpose_adj(0)
-        transpose_adj(1)
-        prepare_x0(1)
-        for c in range(CHUNKS):
-            first_product(0, c)
-            if c + 2 < CHUNKS:
-                transpose_adj(c + 2)
-        for c in range(CHUNKS):
-            first_product(1, c)
-        for b in range(BATCH):
+            prepare_x0(0)
+            transpose_adj(0)
+            transpose_adj(1)
+            prepare_x0(1)
             for c in range(CHUNKS):
-                second_product(b, c)
+                first_product(0, c)
+                if c + 2 < CHUNKS:
+                    transpose_adj(c + 2)
+            for c in range(CHUNKS):
+                first_product(1, c)
+            for b in range(BATCH):
+                for c in range(CHUNKS):
+                    second_product(b, c)

@@ -19,6 +19,7 @@ CHUNKS_PER_PASS = CHUNKS // PASSES
 WORDS = NODES // PAIR
 
 FLOPS = 2 * 2 * NODES * NODES * BATCH * FEATURES
+AHEAD = 3
 
 
 def tile_gts_gcgrucell_pa_kernel(tc, adj, x0, out_0, out_1):
@@ -143,21 +144,21 @@ def tile_gts_gcgrucell_pa_kernel(tc, adj, x0, out_0, out_1):
 
         with tc.manual_schedule():
             load_x0(0)
-            load_adj(0)
-            load_adj(1)
+            for c in range(AHEAD):
+                load_adj(c)
             load_x0(1)
-            load_adj(2)
-            load_adj(3)
+            for c in range(AHEAD, CHUNKS):
+                load_adj(c)
             make_identity(nc, identity[:])
 
             prepare_x0(0)
-            transpose_adj(0)
-            transpose_adj(1)
+            for c in range(AHEAD):
+                transpose_adj(c)
             prepare_x0(1)
             for c in range(CHUNKS):
                 first_product(0, c)
-                if c + 2 < CHUNKS:
-                    transpose_adj(c + 2)
+                if c + AHEAD < CHUNKS:
+                    transpose_adj(c + AHEAD)
             for c in range(CHUNKS):
                 first_product(1, c)
             for b in range(BATCH):

@@ -19,7 +19,7 @@ CHUNKS_PER_PASS = CHUNKS // PASSES
 WORDS = NODES // PAIR
 
 FLOPS = 2 * 2 * NODES * NODES * BATCH * FEATURES
-AHEAD = 3
+RUN = 4
 
 
 def tile_gts_gcgrucell_pa_kernel(tc, adj, x0, out_0, out_1):
@@ -70,15 +70,18 @@ def tile_gts_gcgrucell_pa_kernel(tc, adj, x0, out_0, out_1):
         def regroup(grouped, rows, b, g):
             chunks = slice(g * CHUNKS_PER_PASS, (g + 1) * CHUNKS_PER_PASS)
             nc.vector.tensor_copy(
-                out=grouped[b][:, g], in_=rows[b][:, chunks].rearrange("p u e f -> p f (u e)")
+                out=grouped[b][:, g].rearrange("p (n i) t -> p n t i", i=RUN),
+                in_=rows[b][:, chunks].rearrange("p u e (n i) -> p n (u e) i", i=RUN),
             )
 
         def quantise(grouped, codes, scales):
             nc.vector.quantize_mx(out=codes.bitcast(FP8X4), scales=scales, in_=grouped)
 
-        def prepare_x0(b):
+        def regroup_x0(b):
             for g in range(PASSES):
                 regroup(x0_grouped, x0_rows, b, g)
+
+        def quantise_x0(b):
             quantise(
                 x0_grouped[b][:].rearrange("p g f t -> p (g f t)"),
                 x0_codes[b][:].rearrange("p g f -> p (g f)"),
@@ -144,23 +147,22 @@ def tile_gts_gcgrucell_pa_kernel(tc, adj, x0, out_0, out_1):
 
         with tc.manual_schedule():
             load_x0(0)
-            for c in range(AHEAD):
+            for c in range(CHUNKS):
                 load_adj(c)
             load_x0(1)
-            for c in range(AHEAD, CHUNKS):
-                load_adj(c)
             make_identity(nc, identity[:])
 
-            prepare_x0(0)
-            for c in range(AHEAD):
+            regroup_x0(0)
+            quantise_x0(0)
+            for c in range(CHUNKS - 1):
                 transpose_adj(c)
-            prepare_x0(1)
-            for c in range(CHUNKS):
-                first_product(0, c)
-                if c + AHEAD < CHUNKS:
-                    transpose_adj(c + AHEAD)
-            for c in range(CHUNKS):
-                first_product(1, c)
+            regroup_x0(1)
+            transpose_adj(CHUNKS - 1)
+            quantise_x0(1)
+
+            for b in range(BATCH):
+                for c in range(CHUNKS):
+                    first_product(b, c)
             for b in range(BATCH):
                 for c in range(CHUNKS):
                     second_product(b, c)

@@ -49,10 +49,12 @@ def tile_gts_gcgrucell_pa_kernel(tc, adj, x0, out_0, out_1):
             adj_codes.append(keep.tile([P, PAIR, PASSES, P], U32, name="adj_codes%d" % c, align_bytes=64))
             adj_scales.append(keep.tile([P, PAIR, PASSES, P], U8, name="adj_scales%d" % c, align_bytes=64))
 
-        def load_x0(b):
+        def load_x0(b, g):
+            chunks = slice(g * CHUNKS_PER_PASS, (g + 1) * CHUNKS_PER_PASS)
+            nodes = slice(g * P * PACK, (g + 1) * P * PACK)
             nc.sync.dma_start(
-                out=x0_rows[b][:].rearrange("p c e f -> p c (e f)"),
-                in_=x0[b].rearrange("(c p e) f -> p c (e f)", p=P, e=PAIR),
+                out=x0_rows[b][:, chunks].rearrange("p u e f -> p u (e f)"),
+                in_=x0[b, nodes, :].rearrange("(u p e) f -> p u (e f)", p=P, e=PAIR),
             )
 
         def load_adj(c):
@@ -77,10 +79,6 @@ def tile_gts_gcgrucell_pa_kernel(tc, adj, x0, out_0, out_1):
         def quantise(grouped, codes, scales):
             nc.vector.quantize_mx(out=codes.bitcast(FP8X4), scales=scales, in_=grouped)
 
-        def regroup_x0(b):
-            for g in range(PASSES):
-                regroup(x0_grouped, x0_rows, b, g)
-
         def quantise_x0(b):
             quantise(
                 x0_grouped[b][:].rearrange("p g f t -> p (g f t)"),
@@ -88,24 +86,23 @@ def tile_gts_gcgrucell_pa_kernel(tc, adj, x0, out_0, out_1):
                 x0_scales[b][:].rearrange("p g f -> p (g f)"),
             )
 
-        def transpose_adj(c):
+        def transpose_adj(c, e):
             words = adj_rows[c][:].bitcast(F32)
-            for e in range(PAIR):
-                flipped = psum.tile([P, CHUNKS, P], F32, tag="bank")
-                for j in range(CHUNKS):
-                    first = e * WORDS + j * P
-                    nc.tensor.transpose(flipped[:, j, :], words[:, first : first + P], identity[:])
-                nc.scalar.copy(
-                    out=adj_grouped[c][:, e].bitcast(F32).rearrange(
-                        "p (g r u) -> p g r u", g=PASSES, u=CHUNKS_PER_PASS
-                    ),
-                    in_=flipped[:].rearrange("p (g u) r -> p g r u", u=CHUNKS_PER_PASS),
-                )
-                quantise(
-                    adj_grouped[c][:, e],
-                    adj_codes[c][:, e].rearrange("p g r -> p (g r)"),
-                    adj_scales[c][:, e].rearrange("p g r -> p (g r)"),
-                )
+            flipped = psum.tile([P, CHUNKS, P], F32, tag="bank")
+            for j in range(CHUNKS):
+                first = e * WORDS + j * P
+                nc.tensor.transpose(flipped[:, j, :], words[:, first : first + P], identity[:])
+            nc.scalar.copy(
+                out=adj_grouped[c][:, e].bitcast(F32).rearrange(
+                    "p (g r u) -> p g r u", g=PASSES, u=CHUNKS_PER_PASS
+                ),
+                in_=flipped[:].rearrange("p (g u) r -> p g r u", u=CHUNKS_PER_PASS),
+            )
+            quantise(
+                adj_grouped[c][:, e],
+                adj_codes[c][:, e].rearrange("p g r -> p (g r)"),
+                adj_scales[c][:, e].rearrange("p g r -> p (g r)"),
+            )
 
         def multiply(c, codes, scales):
             product = psum.tile([P, PAIR, FEATURES], F32, tag="bank")
@@ -126,12 +123,9 @@ def tile_gts_gcgrucell_pa_kernel(tc, adj, x0, out_0, out_1):
             product = multiply(c, x0_codes[b], x0_scales[b])
             nc.scalar.copy(out=x1_rows[b][:, c], in_=product[:])
             store(out_0, x1_rows, b, c)
-            if c % CHUNKS_PER_PASS == CHUNKS_PER_PASS - 1:
-                g = c // CHUNKS_PER_PASS
-                regroup(x1_grouped, x1_rows, b, g)
-                quantise(
-                    x1_grouped[b][:, g].rearrange("p f t -> p (f t)"), x1_codes[b][:, g], x1_scales[b][:, g]
-                )
+
+        def quantise_x1(b, g):
+            quantise(x1_grouped[b][:, g].rearrange("p f t -> p (f t)"), x1_codes[b][:, g], x1_scales[b][:, g])
 
         def second_product(b, c):
             product = multiply(c, x1_codes[b], x1_scales[b])
@@ -146,23 +140,40 @@ def tile_gts_gcgrucell_pa_kernel(tc, adj, x0, out_0, out_1):
             store(out_1, x2_rows, b, c)
 
         with tc.manual_schedule():
-            load_x0(0)
+            for g in range(PASSES):
+                load_x0(0, g)
             for c in range(CHUNKS):
                 load_adj(c)
-            load_x0(1)
+            for g in range(PASSES):
+                load_x0(1, g)
             make_identity(nc, identity[:])
 
-            regroup_x0(0)
+            for g in range(PASSES):
+                regroup(x0_grouped, x0_rows, 0, g)
             quantise_x0(0)
             for c in range(CHUNKS - 1):
-                transpose_adj(c)
-            regroup_x0(1)
-            transpose_adj(CHUNKS - 1)
+                for e in range(PAIR):
+                    transpose_adj(c, e)
+            for g, e in zip(range(PASSES), range(PAIR)):
+                regroup(x0_grouped, x0_rows, 1, g)
+                transpose_adj(CHUNKS - 1, e)
             quantise_x0(1)
 
-            for b in range(BATCH):
-                for c in range(CHUNKS):
-                    first_product(b, c)
-            for b in range(BATCH):
-                for c in range(CHUNKS):
-                    second_product(b, c)
+            for c in range(CHUNKS):
+                first_product(0, c)
+                if c % CHUNKS_PER_PASS == CHUNKS_PER_PASS - 1:
+                    regroup(x1_grouped, x1_rows, 0, c // CHUNKS_PER_PASS)
+                    quantise_x1(0, c // CHUNKS_PER_PASS)
+            for c in range(CHUNKS_PER_PASS):
+                first_product(1, c)
+            regroup(x1_grouped, x1_rows, 1, 0)
+            quantise_x1(1, 0)
+            for c in range(CHUNKS_PER_PASS, CHUNKS):
+                first_product(1, c)
+            regroup(x1_grouped, x1_rows, 1, 1)
+            second_product(0, 0)
+            quantise_x1(1, 1)
+            for c in range(1, CHUNKS):
+                second_product(0, c)
+            for c in range(CHUNKS):
+                second_product(1, c)

@@ -20,12 +20,14 @@ WORDS = NODES // PAIR
 
 FLOPS = 2 * 2 * NODES * NODES * BATCH * FEATURES
 RUN = 4
+WARM_UP = 8
 
 
 def tile_gts_gcgrucell_pa_kernel(tc, adj, x0, out_0, out_1):
     nc = tc.nc
     with tc.tile_pool(name="keep", bufs=1) as keep, tc.psum_pool(name="psum", bufs=8) as psum:
         identity = keep.tile([P, P], F32)
+        zeros = keep.tile([P, PACK * P], BF16)
         x0_rows, x1_rows, x2_rows = [], [], []
         x0_grouped, x0_codes, x0_scales = [], [], []
         x1_grouped, x1_codes, x1_scales = [], [], []
@@ -104,6 +106,9 @@ def tile_gts_gcgrucell_pa_kernel(tc, adj, x0, out_0, out_1):
                 adj_scales[c][:, e].rearrange("p g r -> p (g r)"),
             )
 
+        def multiply_zeros(unused):
+            nc.tensor.matmul(out=unused[:], lhsT=zeros[:, :P], rhs=zeros[:], start=True, stop=True)
+
         def multiply(c, codes, scales):
             product = psum.tile([P, PAIR, FEATURES], F32, tag="bank")
             for e in range(PAIR):
@@ -148,12 +153,18 @@ def tile_gts_gcgrucell_pa_kernel(tc, adj, x0, out_0, out_1):
                 load_x0(1, g)
             make_identity(nc, identity[:])
 
+            nc.vector.memset(zeros[:], 0.0)
+            unused = psum.tile([P, PACK * P], F32, tag="bank")
+            for i in range(WARM_UP):
+                multiply_zeros(unused)
+
             for g in range(PASSES):
                 regroup(x0_grouped, x0_rows, 0, g)
             quantise_x0(0)
             for c in range(CHUNKS - 1):
                 for e in range(PAIR):
                     transpose_adj(c, e)
+                multiply_zeros(unused)
             for g, e in zip(range(PASSES), range(PAIR)):
                 regroup(x0_grouped, x0_rows, 1, g)
                 transpose_adj(CHUNKS - 1, e)

import concourse.mybir as mybir
from concourse.masks import make_identity

BF16 = mybir.dt.bfloat16
F32 = mybir.dt.float32
U32 = mybir.dt.uint32
U8 = mybir.dt.uint8
FP8X4 = mybir.dt.float8_e4m3fn_x4

P = 128
PACK = 4
PAIR = 2
NODES = 1024
BATCH = 2
FEATURES = 256
PASSES = NODES // (P * PACK)
CHUNKS = NODES // (P * PAIR)
CHUNKS_PER_PASS = CHUNKS // PASSES
WORDS = NODES // PAIR

FLOPS = 2 * 2 * NODES * NODES * BATCH * FEATURES
RUN = 4
WARM_UP = 8


def tile_gts_gcgrucell_pa_kernel(tc, adj, x0, out_0, out_1):
    nc = tc.nc
    with tc.tile_pool(name="keep", bufs=1) as keep, tc.psum_pool(name="psum", bufs=8) as psum:
        identity = keep.tile([P, P], F32)
        zeros = keep.tile([P, PACK * P], BF16)
        x0_rows, x1_rows, x2_rows = [], [], []
        x0_grouped, x0_codes, x0_scales = [], [], []
        x1_grouped, x1_codes, x1_scales = [], [], []
        for b in range(BATCH):
            x0_rows.append(keep.tile([P, CHUNKS, PAIR, FEATURES], BF16, name="x0_rows%d" % b))
            x1_rows.append(keep.tile([P, CHUNKS, PAIR, FEATURES], F32, name="x1_rows%d" % b))
            x2_rows.append(keep.tile([P, CHUNKS, PAIR, FEATURES], F32, name="x2_rows%d" % b))
            grouped_shape = [P, PASSES, FEATURES, PACK]
            x0_grouped.append(keep.tile(grouped_shape, BF16, name="x0_grouped%d" % b, align_bytes=64))
            x1_grouped.append(keep.tile(grouped_shape, BF16, name="x1_grouped%d" % b, align_bytes=64))
            x0_codes.append(keep.tile([P, PASSES, FEATURES], U32, name="x0_codes%d" % b, align_bytes=64))
            x0_scales.append(keep.tile([P, PASSES, FEATURES], U8, name="x0_scales%d" % b, align_bytes=64))
            x1_codes.append(keep.tile([P, PASSES, FEATURES], U32, name="x1_codes%d" % b, align_bytes=64))
            x1_scales.append(keep.tile([P, PASSES, FEATURES], U8, name="x1_scales%d" % b, align_bytes=64))
        adj_rows, adj_grouped, adj_codes, adj_scales = [], [], [], []
        for c in range(CHUNKS):
            adj_rows.append(keep.tile([P, PAIR * NODES], BF16, name="adj_rows%d" % c))
            adj_grouped.append(
                keep.tile([P, PAIR, PASSES * P * PACK], BF16, name="adj_grouped%d" % c, align_bytes=64)
            )
            adj_codes.append(keep.tile([P, PAIR, PASSES, P], U32, name="adj_codes%d" % c, align_bytes=64))
            adj_scales.append(keep.tile([P, PAIR, PASSES, P], U8, name="adj_scales%d" % c, align_bytes=64))

        def load_x0(b, g):
            chunks = slice(g * CHUNKS_PER_PASS, (g + 1) * CHUNKS_PER_PASS)
            nodes = slice(g * P * PACK, (g + 1) * P * PACK)
            nc.sync.dma_start(
                out=x0_rows[b][:, chunks].rearrange("p u e f -> p u (e f)"),
                in_=x0[b, nodes, :].rearrange("(u p e) f -> p u (e f)", p=P, e=PAIR),
            )

        def load_adj(c):
            nc.sync.dma_start(
                out=adj_rows[c][:],
                in_=adj[c * P * PAIR : (c + 1) * P * PAIR, :].rearrange("(p e) k -> p (e k)", e=PAIR),
            )

        def store(out, rows, b, c):
            nc.sync.dma_start(
                out=out[b, c * P * PAIR : (c + 1) * P * PAIR, :].rearrange("(p e) f -> p (e f)", e=PAIR),
                in_=rows[b][:, c].rearrange("p e f -> p (e f)"),
            )

        def regroup(grouped, rows, b, g):
            chunks = slice(g * CHUNKS_PER_PASS, (g + 1) * CHUNKS_PER_PASS)
            nc.vector.tensor_copy(
                out=grouped[b][:, g].rearrange("p (n i) t -> p n t i", i=RUN),
                in_=rows[b][:, chunks].rearrange("p u e (n i) -> p n (u e) i", i=RUN),
            )

        def quantise(grouped, codes, scales):
            nc.vector.quantize_mx(out=codes.bitcast(FP8X4), scales=scales, in_=grouped)

        def quantise_x0(b):
            quantise(
                x0_grouped[b][:].rearrange("p g f t -> p (g f t)"),
                x0_codes[b][:].rearrange("p g f -> p (g f)"),
                x0_scales[b][:].rearrange("p g f -> p (g f)"),
            )

        def transpose_adj(c, e):
            words = adj_rows[c][:].bitcast(F32)
            flipped = psum.tile([P, CHUNKS, P], F32, tag="bank")
            for j in range(CHUNKS):
                first = e * WORDS + j * P
                nc.tensor.transpose(flipped[:, j, :], words[:, first : first + P], identity[:])
            nc.scalar.copy(
                out=adj_grouped[c][:, e].bitcast(F32).rearrange(
                    "p (g r u) -> p g r u", g=PASSES, u=CHUNKS_PER_PASS
                ),
                in_=flipped[:].rearrange("p (g u) r -> p g r u", u=CHUNKS_PER_PASS),
            )
            quantise(
                adj_grouped[c][:, e],
                adj_codes[c][:, e].rearrange("p g r -> p (g r)"),
                adj_scales[c][:, e].rearrange("p g r -> p (g r)"),
            )

        def multiply_zeros(unused):
            nc.tensor.matmul(out=unused[:], lhsT=zeros[:, :P], rhs=zeros[:], start=True, stop=True)

        def multiply(c, codes, scales):
            product = psum.tile([P, PAIR, FEATURES], F32, tag="bank")
            for e in range(PAIR):
                for g in range(PASSES):
                    nc.tensor.matmul_mx(
                        out=product[:, e, :],
                        lhsT=adj_codes[c][:, e, g, :].bitcast(FP8X4),
                        lhsT_scale=adj_scales[c][:, e, g, :],
                        rhs=codes[:, g, :].bitcast(FP8X4),
                        rhs_scale=scales[:, g, :],
                        start=(g == 0),
                        stop=(g == PASSES - 1),
                    )
            return product

        def first_product(b, c):
            product = multiply(c, x0_codes[b], x0_scales[b])
            nc.scalar.copy(out=x1_rows[b][:, c], in_=product[:])
            store(out_0, x1_rows, b, c)

        def quantise_x1(b, g):
            quantise(x1_grouped[b][:, g].rearrange("p f t -> p (f t)"), x1_codes[b][:, g], x1_scales[b][:, g])

        def second_product(b, c):
            product = multiply(c, x1_codes[b], x1_scales[b])
            nc.vector.scalar_tensor_tensor(
                out=x2_rows[b][:, c],
                in0=product[:],
                scalar=2.0,
                in1=x0_rows[b][:, c],
                op0=mybir.AluOpType.mult,
                op1=mybir.AluOpType.subtract,
            )
            store(out_1, x2_rows, b, c)

        with tc.manual_schedule():
            for g in range(PASSES):
                load_x0(0, g)
            for c in range(CHUNKS):
                load_adj(c)
            for g in range(PASSES):
                load_x0(1, g)
            make_identity(nc, identity[:])

            nc.vector.memset(zeros[:], 0.0)
            unused = psum.tile([P, PACK * P], F32, tag="bank")
            for i in range(WARM_UP):
                multiply_zeros(unused)

            for g in range(PASSES):
                regroup(x0_grouped, x0_rows, 0, g)
            quantise_x0(0)
            for c in range(CHUNKS - 1):
                for e in range(PAIR):
                    transpose_adj(c, e)
                multiply_zeros(unused)
            for g, e in zip(range(PASSES), range(PAIR)):
                regroup(x0_grouped, x0_rows, 1, g)
                transpose_adj(CHUNKS - 1, e)
            quantise_x0(1)

            for c in range(CHUNKS):
                first_product(0, c)
                if c % CHUNKS_PER_PASS == CHUNKS_PER_PASS - 1:
                    regroup(x1_grouped, x1_rows, 0, c // CHUNKS_PER_PASS)
                    quantise_x1(0, c // CHUNKS_PER_PASS)
            for c in range(CHUNKS_PER_PASS):
                first_product(1, c)
            regroup(x1_grouped, x1_rows, 1, 0)
            quantise_x1(1, 0)
            for c in range(CHUNKS_PER_PASS, CHUNKS):
                first_product(1, c)
            regroup(x1_grouped, x1_rows, 1, 1)
            second_product(0, 0)
            quantise_x1(1, 1)
            for c in range(1, CHUNKS):
                second_product(0, c)
            for c in range(CHUNKS):
                second_product(1, c)
